import numpy as np
import ml_dtypes


def mxq(x, axis, fmt="e4m3"):
    dtype, down = {"e4m3": (ml_dtypes.float8_e4m3fn, 7), "e5m2": (ml_dtypes.float8_e5m2, 14)}[fmt]
    v = np.moveaxis(np.asarray(x, np.float32).astype(ml_dtypes.bfloat16).astype(np.float64), axis, -1)
    blocks = v.reshape(v.shape[:-1] + (-1, 32))
    amax = np.abs(blocks).max(-1, keepdims=True)
    byte = np.maximum(np.where(amax > 0, np.frexp(amax)[1] - 1 + 127, 0) - down, 1)
    scale = np.exp2(byte - 127.0)
    codes = (blocks / scale).astype(np.float32).astype(dtype).astype(np.float64)
    return np.moveaxis((codes * scale).reshape(v.shape), -1, axis)


WIDE = False


def mx_kscale(k):
    if not WIDE:
        return np.ones(k)
    levels = np.array([10, -10, 5, -5, 0])
    a = np.random.permutation(np.resize(levels, k // 512 * 4)).reshape(k // 512, 4)
    idx = np.arange(k)
    return np.exp2(a[idx // 512, idx % 128 // 32])


BF16 = ml_dtypes.bfloat16


def bf(x):
    return np.asarray(x, np.float32).astype(BF16)


def f64(x):
    return np.asarray(x).astype(np.float64)


N, V, EN1, EN2, D, K, EMB = 1024, 4096, 1024, 512, 128, 512, 1024
BN_EPS = 1e-5


def batchnorm(x):
    m = x.mean(axis=0)
    v = x.var(axis=0)
    return (x - m) * (1.0 / np.sqrt(v + BN_EPS))


def setup_inputs():
    s, t = mx_kscale(EN1), mx_kscale(EN2)
    return {
        "en1": bf(np.maximum(np.random.standard_normal((N, EN1)) * 1.15, 0.0) * s),
        "W2": bf(np.random.standard_normal((EN1, EN2)) / np.sqrt(EN1) / s[:, None] * t),
        "b2": bf(np.random.standard_normal(EN2) * 0.2 * t),
        "Wmean": bf(np.random.standard_normal((EN2, D)) / np.sqrt(EN2) / t[:, None]),
        "Wlogvar": bf(np.random.standard_normal((EN2, D)) / np.sqrt(EN2) / t[:, None]),
        "eps": bf(np.random.standard_normal((N, D))),
    }


def reference(en1, W2, b2, Wmean, Wlogvar, eps):
    en2 = np.maximum((mxq(f64(en1), 1, "e4m3") @ mxq(f64(W2), 0, "e4m3")) + f64(b2), 0.0)
    en2q = mxq(en2, 1, "e4m3")
    posterior_mean = batchnorm(en2q @ mxq(f64(Wmean), 0, "e4m3"))
    posterior_logvar = batchnorm(en2q @ mxq(f64(Wlogvar), 0, "e4m3"))
    posterior_var = np.exp(posterior_logvar)
    z = posterior_mean + np.sqrt(posterior_var) * f64(eps)
    zx = batchnorm(z)
    return z, zx

@@ -1,0 +1,281 @@
+from contextlib import ExitStack
+
+import concourse.mybir as mybir
+from concourse.masks import make_identity
+
+F32 = mybir.dt.float32
+BF16 = mybir.dt.bfloat16
+U32 = mybir.dt.uint32
+U8 = mybir.dt.uint8
+FP8X4 = mybir.dt.float8_e4m3fn_x4
+ALU = mybir.AluOpType
+ACT = mybir.ActivationFunctionType
+
+P = 128
+PACK = 4
+K_PASS = P * PACK
+
+ROWS, EN1, EN2, D = 1024, 1024, 512, 128
+BN_EPS = 1e-5
+
+CHUNKS = ROWS // P
+BANK = 512
+BANKS = ROWS // BANK
+CHUNKS_PER_BANK = BANK // P
+STAGE = 256
+STAGES = ROWS // STAGE
+CHUNKS_PER_STAGE = STAGE // P
+STAGES_PER_BANK = BANK // STAGE
+PASSES1 = EN1 // K_PASS
+E_TILES = EN2 // P
+HALVES = 2
+RUN = 4
+
+MEAN, LOGVAR, SAMPLE = 0, 1, 2
+BN_STATS_DIM = 6
+
+FLOPS = 2 * ROWS * EN1 * EN2 + 2 * 2 * ROWS * EN2 * D
+
+
+def regroup(copy, grouped, planes):
+    copy(
+        out=grouped.rearrange("p (c i) t -> p c t i", i=RUN),
+        in_=planes.rearrange("p t (c i) -> p c t i", i=RUN),
+    )
+
+
+def tile_modelvd_pa_kernel(tc, en1, W2, b2, Wmean, Wlogvar, eps, out_0, out_1):
+    nc = tc.nc
+    with ExitStack() as ctx:
+        keep = ctx.enter_context(tc.tile_pool(name="keep", bufs=1))
+        stage_pool = ctx.enter_context(tc.tile_pool(name="stage_pool", bufs=2))
+        psum_flip = ctx.enter_context(tc.psum_pool(name="psum_flip", bufs=4))
+        psum_acc = ctx.enter_context(tc.psum_pool(name="psum_acc", bufs=4))
+
+        ident_f32 = keep.tile([P, P], F32)
+        make_identity(nc, ident_f32[:])
+        ident_bf16 = keep.tile([P, P], BF16)
+        make_identity(nc, ident_bf16[:])
+        minus_half = keep.tile([P, 1], F32)
+        nc.vector.memset(minus_half[:], -0.5)
+        table_warmer = keep.tile([P, 1], F32)
+        nc.scalar.activation(out=table_warmer[:], in_=minus_half[:], func=ACT.Exp)
+        b2_rows = keep.tile([P, P], BF16)
+        nc.vector.memset(b2_rows[:], 0.0)
+
+        nc.sync.dma_start(out=b2_rows[0:E_TILES, :], in_=b2.rearrange("(t p) -> t p", p=P))
+        w2_raw = keep.tile([P, PASSES1, PACK, EN2], BF16)
+        for g in range(PASSES1):
+            nc.sync.dma_start(
+                out=w2_raw[:, g].rearrange("q (u e) c -> q u e c", u=HALVES),
+                in_=W2[g * K_PASS : (g + 1) * K_PASS, :].rearrange("(u q e) c -> q u e c", u=HALVES, q=P),
+            )
+        en1_sb = keep.tile([P, CHUNKS, EN1], BF16)
+        en1_rows = en1.rearrange("(p c) k -> p c k", c=CHUNKS)
+        head_raw = keep.tile([P, 2, PACK, D], BF16)
+        eps_sb = keep.tile([P, CHUNKS, D], BF16)
+
+        def load_en1(s):
+            chunks = slice(s * CHUNKS_PER_STAGE, (s + 1) * CHUNKS_PER_STAGE)
+            nc.sync.dma_start(out=en1_sb[:, chunks, :], in_=en1_rows[:, chunks, :])
+
+        load_en1(0)
+        load_en1(1)
+        nc.sync.dma_start(out=head_raw[:, MEAN], in_=Wmean.rearrange("(t p) d -> p t d", p=P))
+        nc.sync.dma_start(out=head_raw[:, LOGVAR], in_=Wlogvar.rearrange("(t p) d -> p t d", p=P))
+        load_en1(2)
+        load_en1(3)
+        nc.sync.dma_start(out=eps_sb[:], in_=eps.rearrange("(p c) d -> p c d", c=CHUNKS))
+
+        b2_flipped = psum_flip.tile([P, P], BF16, tag="flip")
+        nc.tensor.transpose(b2_flipped[:], b2_rows[:], ident_bf16[:])
+        b2_col = keep.tile([P, E_TILES], F32)
+        nc.vector.tensor_copy(out=b2_col[:], in_=b2_flipped[:, 0:E_TILES])
+
+        w2_grouped = keep.tile([P, PASSES1, EN2, PACK], BF16, align_bytes=64)
+        w2_codes = keep.tile([P, PASSES1, EN2], U32, align_bytes=64)
+        w2_scales = keep.tile([P, PASSES1, EN2], U8, align_bytes=64)
+        half = EN2 // 2
+        for g in range(PASSES1):
+            regroup(nc.vector.tensor_copy, w2_grouped[:, g, 0:half, :], w2_raw[:, g, :, 0:half])
+            regroup(nc.scalar.copy, w2_grouped[:, g, half:EN2, :], w2_raw[:, g, :, half:EN2])
+        for g in range(PASSES1):
+            nc.vector.quantize_mx(
+                out=w2_codes[:, g, :].bitcast(FP8X4),
+                scales=w2_scales[:, g, :],
+                in_=w2_grouped[:, g].rearrange("q c t -> q (c t)"),
+            )
+
+        head_codes = keep.tile([P, 2, D], U32, align_bytes=64)
+        head_scales = keep.tile([P, 2, D], U8, align_bytes=64)
+
+        def quantise_head_weights():
+            head_grouped = keep.tile([P, 2, D, PACK], BF16, align_bytes=64)
+            for w in (MEAN, LOGVAR):
+                regroup(nc.vector.tensor_copy, head_grouped[:, w], head_raw[:, w])
+            nc.vector.quantize_mx(
+                out=head_codes[:].rearrange("p w d -> p (w d)").bitcast(FP8X4),
+                scales=head_scales[:].rearrange("p w d -> p (w d)"),
+                in_=head_grouped[:].rearrange("p w d t -> p (w d t)"),
+            )
+
+        en1_codes = keep.tile([P, PASSES1, ROWS], U32, align_bytes=64)
+        en1_scales = keep.tile([P, PASSES1, ROWS], U8, align_bytes=64)
+        en2_codes = keep.tile([P, ROWS], U32, align_bytes=64)
+        en2_scales = keep.tile([P, ROWS], U8, align_bytes=64)
+        stats = keep.tile([P, 3, BANKS, BN_STATS_DIM], F32)
+        head_out = {}
+
+        def flip_and_quantise_en1(s):
+            en1_grouped = stage_pool.tile([P, PASSES1, STAGE, PACK], BF16, align_bytes=64)
+            for i in range(CHUNKS_PER_STAGE):
+                words = en1_sb[:, s * CHUNKS_PER_STAGE + i, :].bitcast(F32)
+                flipped = psum_flip.tile([P, PASSES1, HALVES, P], F32, tag="flip")
+                for g in range(PASSES1):
+                    for u in range(HALVES):
+                        first = (g * HALVES + u) * P
+                        nc.tensor.transpose(flipped[:, g, u, :], words[:, first : first + P], ident_f32[:])
+                nc.scalar.copy(
+                    out=en1_grouped[:, :, i * P : (i + 1) * P, :].bitcast(F32),
+                    in_=flipped[:].rearrange("q g u n -> q g n u"),
+                )
+            stage_cols = slice(s * STAGE, (s + 1) * STAGE)
+            for g in range(PASSES1):
+                nc.vector.quantize_mx(
+                    out=en1_codes[:, g, stage_cols].bitcast(FP8X4),
+                    scales=en1_scales[:, g, stage_cols],
+                    in_=en1_grouped[:, g].rearrange("q n t -> q (n t)"),
+                )
+
+        def hidden_layer(s):
+            stage_cols = slice(s * STAGE, (s + 1) * STAGE)
+            en2_planes = stage_pool.tile([P, E_TILES, STAGE], BF16)
+            for t in range(E_TILES):
+                e_cols = slice(t * P, (t + 1) * P)
+                acc = psum_acc.tile([P, STAGE], F32, tag="acc")
+                for g in range(PASSES1):
+                    nc.tensor.matmul_mx(
+                        out=acc[:],
+                        lhsT=w2_codes[:, g, e_cols].bitcast(FP8X4),
+                        lhsT_scale=w2_scales[:, g, e_cols],
+                        rhs=en1_codes[:, g, stage_cols].bitcast(FP8X4),
+                        rhs_scale=en1_scales[:, g, stage_cols],
+                        start=(g == 0),
+                        stop=(g == PASSES1 - 1),
+                    )
+                nc.scalar.activation(
+                    out=en2_planes[:, t, :], in_=acc[:], func=ACT.Relu, bias=b2_col[:, t : t + 1], scale=1.0
+                )
+            en2_grouped = stage_pool.tile([P, STAGE, PACK], BF16, align_bytes=64)
+            regroup(nc.vector.tensor_copy, en2_grouped[:], en2_planes[:])
+            nc.vector.quantize_mx(
+                out=en2_codes[:, stage_cols].bitcast(FP8X4),
+                scales=en2_scales[:, stage_cols],
+                in_=en2_grouped[:].rearrange("p n t -> p (n t)"),
+            )
+
+        def heads(s):
+            stage_cols = slice(s * STAGE, (s + 1) * STAGE)
+            b, part = divmod(s, STAGES_PER_BANK)
+            for w in (MEAN, LOGVAR):
+                nc.tensor.matmul_mx(
+                    out=head_out[(w, b)][:, part * STAGE : (part + 1) * STAGE],
+                    lhsT=head_codes[:, w, :].bitcast(FP8X4),
+                    lhsT_scale=head_scales[:, w, :],
+                    rhs=en2_codes[:, stage_cols].bitcast(FP8X4),
+                    rhs_scale=en2_scales[:, stage_cols],
+                    start=True,
+                    stop=True,
+                )
+            if part == STAGES_PER_BANK - 1:
+                for w in (MEAN, LOGVAR):
+                    nc.vector.bn_stats(out=stats[:, w, b, :], in_=head_out[(w, b)][:])
+
+        flip_and_quantise_en1(0)
+        flip_and_quantise_en1(1)
+        quantise_head_weights()
+        hidden_layer(0)
+        flip_and_quantise_en1(2)
+        hidden_layer(1)
+        flip_and_quantise_en1(3)
+        hidden_layer(2)
+        for b in range(BANKS):
+            for w in (MEAN, LOGVAR):
+                head_out[(w, b)] = psum_flip.tile([P, BANK], F32, name="head_out%d%d" % (w, b), tag="flip")
+        heads(0)
+        heads(1)
+        hidden_layer(3)
+        heads(2)
+        eps_flipped = psum_acc.tile([P, CHUNKS, P], BF16, tag="acc")
+        for c in range(CHUNKS):
+            nc.tensor.transpose(eps_flipped[:, c, :], eps_sb[:, c, :], ident_bf16[:])
+        heads(3)
+
+        def mean_and_inverse_std(which, factor):
+            mean_var = keep.tile([P, 2], F32, name="mean_var%d" % which)
+            nc.vector.bn_aggr(out=mean_var[:], in_=stats[:, which].rearrange("p b s -> p (b s)"))
+            shifted = keep.tile([P, 1], F32, name="shifted%d" % which)
+            nc.vector.tensor_scalar(
+                out=shifted[:], in0=mean_var[:, 1:2], scalar1=BN_EPS, scalar2=factor, op0=ALU.add, op1=ALU.mult
+            )
+            inv = keep.tile([P, 1], F32, name="inv%d" % which)
+            nc.gpsimd.tensor_tensor(out=inv[:], in0=shifted[:], in1=minus_half[:], op=ALU.pow)
+            return mean_var, inv
+
+        def normalise(out, in_, mean_var, inv):
+            nc.vector.tensor_scalar(
+                out=out, in0=in_, scalar1=mean_var[:, 0:1], scalar2=inv[:], op0=ALU.subtract, op1=ALU.mult
+            )
+
+        def store_rows(values_t, b, copy, out):
+            back = psum_acc.tile([P, CHUNKS_PER_BANK, D], F32, tag="acc")
+            for i in range(CHUNKS_PER_BANK):
+                first = (b * CHUNKS_PER_BANK + i) * P
+                nc.tensor.transpose(back[:, i, :], values_t[:, first : first + P], ident_f32[:])
+            rows = stage_pool.tile([P, CHUNKS_PER_BANK, D], F32)
+            copy(out=rows[:], in_=back[:])
+            chunks = slice(b * CHUNKS_PER_BANK, (b + 1) * CHUNKS_PER_BANK)
+            nc.sync.dma_start(out=out.rearrange("(p c) d -> p c d", c=CHUNKS)[:, chunks, :], in_=rows[:])
+
+        std_t = keep.tile([P, ROWS], F32)
+        m_t = keep.tile([P, ROWS], F32)
+        z_t = keep.tile([P, ROWS], F32)
+        zx_t = keep.tile([P, ROWS], F32)
+        bank_cols = [slice(b * BANK, (b + 1) * BANK) for b in range(BANKS)]
+
+        m_mean_var, m_inv = mean_and_inverse_std(MEAN, 1.0)
+        lv_mean_var, lv_half_inv = mean_and_inverse_std(LOGVAR, 4.0)
+        normalise(m_t[:, bank_cols[0]], head_out[(MEAN, 0)][:], m_mean_var, m_inv)
+        exp_bias = keep.tile([P, 1], F32)
+        nc.vector.scalar_tensor_tensor(
+            out=exp_bias[:], in0=lv_mean_var[:, 0:1], scalar=-1.0, in1=lv_half_inv[:], op0=ALU.mult, op1=ALU.mult
+        )
+        for b in range(BANKS):
+            nc.scalar.activation(
+                out=std_t[:, bank_cols[b]],
+                in_=head_out[(LOGVAR, b)][:],
+                func=ACT.Exp,
+                bias=exp_bias[:],
+                scale=lv_half_inv[:],
+            )
+        normalise(m_t[:, bank_cols[1]], head_out[(MEAN, 1)][:], m_mean_var, m_inv)
+
+        for b in range(BANKS):
+            chunks = slice(b * CHUNKS_PER_BANK, (b + 1) * CHUNKS_PER_BANK)
+            nc.vector.tensor_tensor(
+                out=std_t[:, bank_cols[b]],
+                in0=std_t[:, bank_cols[b]],
+                in1=eps_flipped[:, chunks, :].rearrange("d c n -> d (c n)"),
+                op=ALU.mult,
+            )
+            nc.vector.tensor_tensor(
+                out=z_t[:, bank_cols[b]], in0=std_t[:, bank_cols[b]], in1=m_t[:, bank_cols[b]], op=ALU.add
+            )
+            nc.vector.bn_stats(out=stats[:, SAMPLE, b, :], in_=z_t[:, bank_cols[b]])
+            store_rows(z_t, b, nc.scalar.copy, out_0)
+
+        z_mean_var, z_inv = mean_and_inverse_std(SAMPLE, 1.0)
+        for b in range(BANKS):
+            normalise(zx_t[:, bank_cols[b]], z_t[:, bank_cols[b]], z_mean_var, z_inv)
+        store_rows(zx_t, 0, nc.scalar.copy, out_1)
+        store_rows(zx_t, 1, nc.vector.tensor_copy, out_1)

@@ -49,6 +49,7 @@ def tile_modelvd_pa_kernel(tc, en1, W2, b2, Wmean, Wlogvar, eps, out_0, out_1):
     with ExitStack() as ctx:
         keep = ctx.enter_context(tc.tile_pool(name="keep", bufs=1))
         stage_pool = ctx.enter_context(tc.tile_pool(name="stage_pool", bufs=2))
+        rows_pool = ctx.enter_context(tc.tile_pool(name="rows_pool", bufs=2 * BANKS))
         psum_flip = ctx.enter_context(tc.psum_pool(name="psum_flip", bufs=4))
         psum_acc = ctx.enter_context(tc.psum_pool(name="psum_acc", bufs=4))
 
@@ -188,8 +189,7 @@ def tile_modelvd_pa_kernel(tc, en1, W2, b2, Wmean, Wlogvar, eps, out_0, out_1):
                     stop=True,
                 )
             if part == STAGES_PER_BANK - 1:
-                for w in (MEAN, LOGVAR):
-                    nc.vector.bn_stats(out=stats[:, w, b, :], in_=head_out[(w, b)][:])
+                nc.vector.bn_stats(out=stats[:, LOGVAR, b, :], in_=head_out[(LOGVAR, b)][:])
 
         flip_and_quantise_en1(0)
         flip_and_quantise_en1(1)
@@ -211,71 +211,90 @@ def tile_modelvd_pa_kernel(tc, en1, W2, b2, Wmean, Wlogvar, eps, out_0, out_1):
             nc.tensor.transpose(eps_flipped[:, c, :], eps_sb[:, c, :], ident_bf16[:])
         heads(3)
 
-        def mean_and_inverse_std(which, factor):
+        def mean_and_inverse_std(which, stats, epsilon, factor):
             mean_var = keep.tile([P, 2], F32, name="mean_var%d" % which)
-            nc.vector.bn_aggr(out=mean_var[:], in_=stats[:, which].rearrange("p b s -> p (b s)"))
+            nc.vector.bn_aggr(out=mean_var[:], in_=stats.rearrange("p b s -> p (b s)"))
             shifted = keep.tile([P, 1], F32, name="shifted%d" % which)
             nc.vector.tensor_scalar(
-                out=shifted[:], in0=mean_var[:, 1:2], scalar1=BN_EPS, scalar2=factor, op0=ALU.add, op1=ALU.mult
+                out=shifted[:], in0=mean_var[:, 1:2], scalar1=epsilon, scalar2=factor, op0=ALU.add, op1=ALU.mult
             )
             inv = keep.tile([P, 1], F32, name="inv%d" % which)
             nc.gpsimd.tensor_tensor(out=inv[:], in0=shifted[:], in1=minus_half[:], op=ALU.pow)
-            return mean_var, inv
-
-        def normalise(out, in_, mean_var, inv):
-            nc.vector.tensor_scalar(
-                out=out, in0=in_, scalar1=mean_var[:, 0:1], scalar2=inv[:], op0=ALU.subtract, op1=ALU.mult
-            )
+            return mean_var, shifted, inv
 
         def store_rows(values_t, b, copy, out):
             back = psum_acc.tile([P, CHUNKS_PER_BANK, D], F32, tag="acc")
             for i in range(CHUNKS_PER_BANK):
                 first = (b * CHUNKS_PER_BANK + i) * P
                 nc.tensor.transpose(back[:, i, :], values_t[:, first : first + P], ident_f32[:])
-            rows = stage_pool.tile([P, CHUNKS_PER_BANK, D], F32)
+            rows = rows_pool.tile([P, CHUNKS_PER_BANK, D], F32)
             copy(out=rows[:], in_=back[:])
             chunks = slice(b * CHUNKS_PER_BANK, (b + 1) * CHUNKS_PER_BANK)
             nc.sync.dma_start(out=out.rearrange("(p c) d -> p c d", c=CHUNKS)[:, chunks, :], in_=rows[:])
 
-        std_t = keep.tile([P, ROWS], F32)
-        m_t = keep.tile([P, ROWS], F32)
+        noise_t = keep.tile([P, ROWS], F32)
+        y_t = keep.tile([P, ROWS], F32)
         z_t = keep.tile([P, ROWS], F32)
         zx_t = keep.tile([P, ROWS], F32)
         bank_cols = [slice(b * BANK, (b + 1) * BANK) for b in range(BANKS)]
 
-        m_mean_var, m_inv = mean_and_inverse_std(MEAN, 1.0)
-        lv_mean_var, lv_half_inv = mean_and_inverse_std(LOGVAR, 4.0)
-        normalise(m_t[:, bank_cols[0]], head_out[(MEAN, 0)][:], m_mean_var, m_inv)
+        lv_mean_var, lv_shifted, lv_half_inv = mean_and_inverse_std(LOGVAR, stats[:, LOGVAR], BN_EPS, 4.0)
+        lv_minus_mean = keep.tile([P, 1], F32)
+        nc.vector.tensor_scalar_mul(out=lv_minus_mean[:], in0=lv_mean_var[:, 0:1], scalar1=-1.0)
         exp_bias = keep.tile([P, 1], F32)
-        nc.vector.scalar_tensor_tensor(
-            out=exp_bias[:], in0=lv_mean_var[:, 0:1], scalar=-1.0, in1=lv_half_inv[:], op0=ALU.mult, op1=ALU.mult
-        )
+        nc.scalar.activation(out=exp_bias[:], in_=lv_minus_mean[:], func=ACT.Copy, scale=lv_half_inv[:])
         for b in range(BANKS):
             nc.scalar.activation(
-                out=std_t[:, bank_cols[b]],
+                out=noise_t[:, bank_cols[b]],
                 in_=head_out[(LOGVAR, b)][:],
                 func=ACT.Exp,
                 bias=exp_bias[:],
                 scale=lv_half_inv[:],
             )
-        normalise(m_t[:, bank_cols[1]], head_out[(MEAN, 1)][:], m_mean_var, m_inv)
+
+        for b in range(BANKS):
+            nc.vector.bn_stats(out=stats[:, MEAN, b, :], in_=head_out[(MEAN, b)][:])
+        m_mean_var, m_shifted, m_inv = mean_and_inverse_std(MEAN, stats[:, MEAN], BN_EPS, 1.0)
+        m_sd = keep.tile([P, 1], F32)
+        nc.vector.tensor_tensor(out=m_sd[:], in0=m_shifted[:], in1=m_inv[:], op=ALU.mult)
+        y_epsilon = keep.tile([P, 1], F32)
+        nc.vector.tensor_scalar_mul(out=y_epsilon[:], in0=m_shifted[:], scalar1=BN_EPS)
+        z_bias = keep.tile([P, 1], F32)
+        nc.vector.scalar_tensor_tensor(
+            out=z_bias[:], in0=m_mean_var[:, 0:1], scalar=-1.0, in1=m_inv[:], op0=ALU.mult, op1=ALU.mult
+        )
 
         for b in range(BANKS):
             chunks = slice(b * CHUNKS_PER_BANK, (b + 1) * CHUNKS_PER_BANK)
             nc.vector.tensor_tensor(
-                out=std_t[:, bank_cols[b]],
-                in0=std_t[:, bank_cols[b]],
+                out=noise_t[:, bank_cols[b]],
+                in0=noise_t[:, bank_cols[b]],
                 in1=eps_flipped[:, chunks, :].rearrange("d c n -> d (c n)"),
                 op=ALU.mult,
             )
-            nc.vector.tensor_tensor(
-                out=z_t[:, bank_cols[b]], in0=std_t[:, bank_cols[b]], in1=m_t[:, bank_cols[b]], op=ALU.add
+            nc.vector.scalar_tensor_tensor(
+                out=y_t[:, bank_cols[b]],
+                in0=noise_t[:, bank_cols[b]],
+                scalar=m_sd[:],
+                in1=head_out[(MEAN, b)][:],
+                op0=ALU.mult,
+                op1=ALU.add,
             )
-            nc.vector.bn_stats(out=stats[:, SAMPLE, b, :], in_=z_t[:, bank_cols[b]])
+            nc.vector.bn_stats(out=stats[:, SAMPLE, b, :], in_=y_t[:, bank_cols[b]])
+            nc.scalar.activation(
+                out=z_t[:, bank_cols[b]], in_=y_t[:, bank_cols[b]], func=ACT.Identity, bias=z_bias[:], scale=m_inv[:]
+            )
             store_rows(z_t, b, nc.scalar.copy, out_0)
 
-        z_mean_var, z_inv = mean_and_inverse_std(SAMPLE, 1.0)
+        y_mean_var, y_shifted, y_inv = mean_and_inverse_std(SAMPLE, stats[:, SAMPLE], y_epsilon[:], 1.0)
         for b in range(BANKS):
-            normalise(zx_t[:, bank_cols[b]], z_t[:, bank_cols[b]], z_mean_var, z_inv)
+            nc.vector.tensor_scalar(
+                out=zx_t[:, bank_cols[b]],
+                in0=y_t[:, bank_cols[b]],
+                scalar1=y_mean_var[:, 0:1],
+                scalar2=y_inv[:],
+                op0=ALU.subtract,
+                op1=ALU.mult,
+            )
         store_rows(zx_t, 0, nc.scalar.copy, out_1)
         store_rows(zx_t, 1, nc.vector.tensor_copy, out_1)

@@ -47,6 +47,7 @@ def regroup(copy, grouped, planes):
 def tile_modelvd_pa_kernel(tc, en1, W2, b2, Wmean, Wlogvar, eps, out_0, out_1):
     nc = tc.nc
     with ExitStack() as ctx:
+        ctx.enter_context(tc.manual_schedule())
         keep = ctx.enter_context(tc.tile_pool(name="keep", bufs=1))
         stage_pool = ctx.enter_context(tc.tile_pool(name="stage_pool", bufs=2))
         rows_pool = ctx.enter_context(tc.tile_pool(name="rows_pool", bufs=2 * BANKS))
@@ -64,13 +65,13 @@ def tile_modelvd_pa_kernel(tc, en1, W2, b2, Wmean, Wlogvar, eps, out_0, out_1):
         b2_rows = keep.tile([P, P], BF16)
         nc.vector.memset(b2_rows[:], 0.0)
 
-        nc.sync.dma_start(out=b2_rows[0:E_TILES, :], in_=b2.rearrange("(t p) -> t p", p=P))
         w2_raw = keep.tile([P, PASSES1, PACK, EN2], BF16)
         for g in range(PASSES1):
             nc.sync.dma_start(
                 out=w2_raw[:, g].rearrange("q (u e) c -> q u e c", u=HALVES),
                 in_=W2[g * K_PASS : (g + 1) * K_PASS, :].rearrange("(u q e) c -> q u e c", u=HALVES, q=P),
             )
+        nc.sync.dma_start(out=b2_rows[0:E_TILES, :], in_=b2.rearrange("(t p) -> t p", p=P))
         en1_sb = keep.tile([P, CHUNKS, EN1], BF16)
         en1_rows = en1.rearrange("(p c) k -> p c k", c=CHUNKS)
         head_raw = keep.tile([P, 2, PACK, D], BF16)
@@ -87,11 +88,6 @@ def tile_modelvd_pa_kernel(tc, en1, W2, b2, Wmean, Wlogvar, eps, out_0, out_1):
         load_en1(2)
         load_en1(3)
         nc.sync.dma_start(out=eps_sb[:], in_=eps.rearrange("(p c) d -> p c d", c=CHUNKS))
-
-        b2_flipped = psum_flip.tile([P, P], BF16, tag="flip")
-        nc.tensor.transpose(b2_flipped[:], b2_rows[:], ident_bf16[:])
-        b2_col = keep.tile([P, E_TILES], F32)
-        nc.vector.tensor_copy(out=b2_col[:], in_=b2_flipped[:, 0:E_TILES])
 
         w2_grouped = keep.tile([P, PASSES1, EN2, PACK], BF16, align_bytes=64)
         w2_codes = keep.tile([P, PASSES1, EN2], U32, align_bytes=64)
@@ -192,17 +188,21 @@ def tile_modelvd_pa_kernel(tc, en1, W2, b2, Wmean, Wlogvar, eps, out_0, out_1):
                 nc.vector.bn_stats(out=stats[:, LOGVAR, b, :], in_=head_out[(LOGVAR, b)][:])
 
         flip_and_quantise_en1(0)
+        b2_flipped = psum_flip.tile([P, P], BF16, tag="flip")
+        nc.tensor.transpose(b2_flipped[:], b2_rows[:], ident_bf16[:])
+        b2_col = keep.tile([P, E_TILES], F32)
+        nc.vector.tensor_copy(out=b2_col[:], in_=b2_flipped[:, 0:E_TILES])
         flip_and_quantise_en1(1)
         quantise_head_weights()
         hidden_layer(0)
         flip_and_quantise_en1(2)
         hidden_layer(1)
         flip_and_quantise_en1(3)
-        hidden_layer(2)
         for b in range(BANKS):
             for w in (MEAN, LOGVAR):
                 head_out[(w, b)] = psum_flip.tile([P, BANK], F32, name="head_out%d%d" % (w, b), tag="flip")
         heads(0)
+        hidden_layer(2)
         heads(1)
         hidden_layer(3)
         heads(2)
@@ -255,15 +255,6 @@ def tile_modelvd_pa_kernel(tc, en1, W2, b2, Wmean, Wlogvar, eps, out_0, out_1):
         for b in range(BANKS):
             nc.vector.bn_stats(out=stats[:, MEAN, b, :], in_=head_out[(MEAN, b)][:])
         m_mean_var, m_shifted, m_inv = mean_and_inverse_std(MEAN, stats[:, MEAN], BN_EPS, 1.0)
-        m_sd = keep.tile([P, 1], F32)
-        nc.vector.tensor_tensor(out=m_sd[:], in0=m_shifted[:], in1=m_inv[:], op=ALU.mult)
-        y_epsilon = keep.tile([P, 1], F32)
-        nc.vector.tensor_scalar_mul(out=y_epsilon[:], in0=m_shifted[:], scalar1=BN_EPS)
-        z_bias = keep.tile([P, 1], F32)
-        nc.vector.scalar_tensor_tensor(
-            out=z_bias[:], in0=m_mean_var[:, 0:1], scalar=-1.0, in1=m_inv[:], op0=ALU.mult, op1=ALU.mult
-        )
-
         for b in range(BANKS):
             chunks = slice(b * CHUNKS_PER_BANK, (b + 1) * CHUNKS_PER_BANK)
             nc.vector.tensor_tensor(
@@ -272,6 +263,15 @@ def tile_modelvd_pa_kernel(tc, en1, W2, b2, Wmean, Wlogvar, eps, out_0, out_1):
                 in1=eps_flipped[:, chunks, :].rearrange("d c n -> d (c n)"),
                 op=ALU.mult,
             )
+        m_sd = keep.tile([P, 1], F32)
+        nc.vector.tensor_tensor(out=m_sd[:], in0=m_shifted[:], in1=m_inv[:], op=ALU.mult)
+        y_epsilon = keep.tile([P, 1], F32)
+        nc.vector.tensor_scalar_mul(out=y_epsilon[:], in0=m_shifted[:], scalar1=BN_EPS)
+        z_bias = keep.tile([P, 1], F32)
+        nc.vector.scalar_tensor_tensor(
+            out=z_bias[:], in0=m_mean_var[:, 0:1], scalar=-1.0, in1=m_inv[:], op0=ALU.mult, op1=ALU.mult
+        )
+        for b in range(BANKS):
             nc.vector.scalar_tensor_tensor(
                 out=y_t[:, bank_cols[b]],
                 in0=noise_t[:, bank_cols[b]],

from contextlib import ExitStack

import concourse.mybir as mybir
from concourse.masks import make_identity

F32 = mybir.dt.float32
BF16 = mybir.dt.bfloat16
U32 = mybir.dt.uint32
U8 = mybir.dt.uint8
FP8X4 = mybir.dt.float8_e4m3fn_x4
ALU = mybir.AluOpType
ACT = mybir.ActivationFunctionType

P = 128
PACK = 4
K_PASS = P * PACK

ROWS, EN1, EN2, D = 1024, 1024, 512, 128
BN_EPS = 1e-5

CHUNKS = ROWS // P
BANK = 512
BANKS = ROWS // BANK
CHUNKS_PER_BANK = BANK // P
STAGE = 256
STAGES = ROWS // STAGE
CHUNKS_PER_STAGE = STAGE // P
STAGES_PER_BANK = BANK // STAGE
PASSES1 = EN1 // K_PASS
E_TILES = EN2 // P
HALVES = 2
RUN = 4

MEAN, LOGVAR, SAMPLE = 0, 1, 2
BN_STATS_DIM = 6

FLOPS = 2 * ROWS * EN1 * EN2 + 2 * 2 * ROWS * EN2 * D


def regroup(copy, grouped, planes):
    copy(
        out=grouped.rearrange("p (c i) t -> p c t i", i=RUN),
        in_=planes.rearrange("p t (c i) -> p c t i", i=RUN),
    )


def tile_modelvd_pa_kernel(tc, en1, W2, b2, Wmean, Wlogvar, eps, out_0, out_1):
    nc = tc.nc
    with ExitStack() as ctx:
        ctx.enter_context(tc.manual_schedule())
        keep = ctx.enter_context(tc.tile_pool(name="keep", bufs=1))
        stage_pool = ctx.enter_context(tc.tile_pool(name="stage_pool", bufs=2))
        rows_pool = ctx.enter_context(tc.tile_pool(name="rows_pool", bufs=2 * BANKS))
        psum_flip = ctx.enter_context(tc.psum_pool(name="psum_flip", bufs=4))
        psum_acc = ctx.enter_context(tc.psum_pool(name="psum_acc", bufs=4))

        ident_f32 = keep.tile([P, P], F32)
        make_identity(nc, ident_f32[:])
        ident_bf16 = keep.tile([P, P], BF16)
        make_identity(nc, ident_bf16[:])
        minus_half = keep.tile([P, 1], F32)
        nc.vector.memset(minus_half[:], -0.5)
        table_warmer = keep.tile([P, 1], F32)
        nc.scalar.activation(out=table_warmer[:], in_=minus_half[:], func=ACT.Exp)
        b2_rows = keep.tile([P, P], BF16)
        nc.vector.memset(b2_rows[:], 0.0)

        w2_raw = keep.tile([P, PASSES1, PACK, EN2], BF16)
        for g in range(PASSES1):
            nc.sync.dma_start(
                out=w2_raw[:, g].rearrange("q (u e) c -> q u e c", u=HALVES),
                in_=W2[g * K_PASS : (g + 1) * K_PASS, :].rearrange("(u q e) c -> q u e c", u=HALVES, q=P),
            )
        nc.sync.dma_start(out=b2_rows[0:E_TILES, :], in_=b2.rearrange("(t p) -> t p", p=P))
        en1_sb = keep.tile([P, CHUNKS, EN1], BF16)
        en1_rows = en1.rearrange("(p c) k -> p c k", c=CHUNKS)
        head_raw = keep.tile([P, 2, PACK, D], BF16)
        eps_sb = keep.tile([P, CHUNKS, D], BF16)

        def load_en1(s):
            chunks = slice(s * CHUNKS_PER_STAGE, (s + 1) * CHUNKS_PER_STAGE)
            nc.sync.dma_start(out=en1_sb[:, chunks, :], in_=en1_rows[:, chunks, :])

        load_en1(0)
        load_en1(1)
        nc.sync.dma_start(out=head_raw[:, MEAN], in_=Wmean.rearrange("(t p) d -> p t d", p=P))
        nc.sync.dma_start(out=head_raw[:, LOGVAR], in_=Wlogvar.rearrange("(t p) d -> p t d", p=P))
        load_en1(2)
        load_en1(3)
        nc.sync.dma_start(out=eps_sb[:], in_=eps.rearrange("(p c) d -> p c d", c=CHUNKS))

        w2_grouped = keep.tile([P, PASSES1, EN2, PACK], BF16, align_bytes=64)
        w2_codes = keep.tile([P, PASSES1, EN2], U32, align_bytes=64)
        w2_scales = keep.tile([P, PASSES1, EN2], U8, align_bytes=64)
        half = EN2 // 2
        for g in range(PASSES1):
            regroup(nc.vector.tensor_copy, w2_grouped[:, g, 0:half, :], w2_raw[:, g, :, 0:half])
            regroup(nc.scalar.copy, w2_grouped[:, g, half:EN2, :], w2_raw[:, g, :, half:EN2])
        for g in range(PASSES1):
            nc.vector.quantize_mx(
                out=w2_codes[:, g, :].bitcast(FP8X4),
                scales=w2_scales[:, g, :],
                in_=w2_grouped[:, g].rearrange("q c t -> q (c t)"),
            )

        head_codes = keep.tile([P, 2, D], U32, align_bytes=64)
        head_scales = keep.tile([P, 2, D], U8, align_bytes=64)

        def quantise_head_weights():
            head_grouped = keep.tile([P, 2, D, PACK], BF16, align_bytes=64)
            for w in (MEAN, LOGVAR):
                regroup(nc.vector.tensor_copy, head_grouped[:, w], head_raw[:, w])
            nc.vector.quantize_mx(
                out=head_codes[:].rearrange("p w d -> p (w d)").bitcast(FP8X4),
                scales=head_scales[:].rearrange("p w d -> p (w d)"),
                in_=head_grouped[:].rearrange("p w d t -> p (w d t)"),
            )

        en1_codes = keep.tile([P, PASSES1, ROWS], U32, align_bytes=64)
        en1_scales = keep.tile([P, PASSES1, ROWS], U8, align_bytes=64)
        en2_codes = keep.tile([P, ROWS], U32, align_bytes=64)
        en2_scales = keep.tile([P, ROWS], U8, align_bytes=64)
        stats = keep.tile([P, 3, BANKS, BN_STATS_DIM], F32)
        head_out = {}

        def flip_and_quantise_en1(s):
            en1_grouped = stage_pool.tile([P, PASSES1, STAGE, PACK], BF16, align_bytes=64)
            for i in range(CHUNKS_PER_STAGE):
                words = en1_sb[:, s * CHUNKS_PER_STAGE + i, :].bitcast(F32)
                flipped = psum_flip.tile([P, PASSES1, HALVES, P], F32, tag="flip")
                for g in range(PASSES1):
                    for u in range(HALVES):
                        first = (g * HALVES + u) * P
                        nc.tensor.transpose(flipped[:, g, u, :], words[:, first : first + P], ident_f32[:])
                nc.scalar.copy(
                    out=en1_grouped[:, :, i * P : (i + 1) * P, :].bitcast(F32),
                    in_=flipped[:].rearrange("q g u n -> q g n u"),
                )
            stage_cols = slice(s * STAGE, (s + 1) * STAGE)
            for g in range(PASSES1):
                nc.vector.quantize_mx(
                    out=en1_codes[:, g, stage_cols].bitcast(FP8X4),
                    scales=en1_scales[:, g, stage_cols],
                    in_=en1_grouped[:, g].rearrange("q n t -> q (n t)"),
                )

        def hidden_layer(s):
            stage_cols = slice(s * STAGE, (s + 1) * STAGE)
            en2_planes = stage_pool.tile([P, E_TILES, STAGE], BF16)
            for t in range(E_TILES):
                e_cols = slice(t * P, (t + 1) * P)
                acc = psum_acc.tile([P, STAGE], F32, tag="acc")
                for g in range(PASSES1):
                    nc.tensor.matmul_mx(
                        out=acc[:],
                        lhsT=w2_codes[:, g, e_cols].bitcast(FP8X4),
                        lhsT_scale=w2_scales[:, g, e_cols],
                        rhs=en1_codes[:, g, stage_cols].bitcast(FP8X4),
                        rhs_scale=en1_scales[:, g, stage_cols],
                        start=(g == 0),
                        stop=(g == PASSES1 - 1),
                    )
                nc.scalar.activation(
                    out=en2_planes[:, t, :], in_=acc[:], func=ACT.Relu, bias=b2_col[:, t : t + 1], scale=1.0
                )
            en2_grouped = stage_pool.tile([P, STAGE, PACK], BF16, align_bytes=64)
            regroup(nc.vector.tensor_copy, en2_grouped[:], en2_planes[:])
            nc.vector.quantize_mx(
                out=en2_codes[:, stage_cols].bitcast(FP8X4),
                scales=en2_scales[:, stage_cols],
                in_=en2_grouped[:].rearrange("p n t -> p (n t)"),
            )

        def heads(s):
            stage_cols = slice(s * STAGE, (s + 1) * STAGE)
            b, part = divmod(s, STAGES_PER_BANK)
            for w in (MEAN, LOGVAR):
                nc.tensor.matmul_mx(
                    out=head_out[(w, b)][:, part * STAGE : (part + 1) * STAGE],
                    lhsT=head_codes[:, w, :].bitcast(FP8X4),
                    lhsT_scale=head_scales[:, w, :],
                    rhs=en2_codes[:, stage_cols].bitcast(FP8X4),
                    rhs_scale=en2_scales[:, stage_cols],
                    start=True,
                    stop=True,
                )
            if part == STAGES_PER_BANK - 1:
                nc.vector.bn_stats(out=stats[:, LOGVAR, b, :], in_=head_out[(LOGVAR, b)][:])

        flip_and_quantise_en1(0)
        b2_flipped = psum_flip.tile([P, P], BF16, tag="flip")
        nc.tensor.transpose(b2_flipped[:], b2_rows[:], ident_bf16[:])
        b2_col = keep.tile([P, E_TILES], F32)
        nc.vector.tensor_copy(out=b2_col[:], in_=b2_flipped[:, 0:E_TILES])
        flip_and_quantise_en1(1)
        quantise_head_weights()
        hidden_layer(0)
        flip_and_quantise_en1(2)
        hidden_layer(1)
        flip_and_quantise_en1(3)
        for b in range(BANKS):
            for w in (MEAN, LOGVAR):
                head_out[(w, b)] = psum_flip.tile([P, BANK], F32, name="head_out%d%d" % (w, b), tag="flip")
        heads(0)
        hidden_layer(2)
        heads(1)
        hidden_layer(3)
        heads(2)
        eps_flipped = psum_acc.tile([P, CHUNKS, P], BF16, tag="acc")
        for c in range(CHUNKS):
            nc.tensor.transpose(eps_flipped[:, c, :], eps_sb[:, c, :], ident_bf16[:])
        heads(3)

        def mean_and_inverse_std(which, stats, epsilon, factor):
            mean_var = keep.tile([P, 2], F32, name="mean_var%d" % which)
            nc.vector.bn_aggr(out=mean_var[:], in_=stats.rearrange("p b s -> p (b s)"))
            shifted = keep.tile([P, 1], F32, name="shifted%d" % which)
            nc.vector.tensor_scalar(
                out=shifted[:], in0=mean_var[:, 1:2], scalar1=epsilon, scalar2=factor, op0=ALU.add, op1=ALU.mult
            )
            inv = keep.tile([P, 1], F32, name="inv%d" % which)
            nc.gpsimd.tensor_tensor(out=inv[:], in0=shifted[:], in1=minus_half[:], op=ALU.pow)
            return mean_var, shifted, inv

        def store_rows(values_t, b, copy, out):
            back = psum_acc.tile([P, CHUNKS_PER_BANK, D], F32, tag="acc")
            for i in range(CHUNKS_PER_BANK):
                first = (b * CHUNKS_PER_BANK + i) * P
                nc.tensor.transpose(back[:, i, :], values_t[:, first : first + P], ident_f32[:])
            rows = rows_pool.tile([P, CHUNKS_PER_BANK, D], F32)
            copy(out=rows[:], in_=back[:])
            chunks = slice(b * CHUNKS_PER_BANK, (b + 1) * CHUNKS_PER_BANK)
            nc.sync.dma_start(out=out.rearrange("(p c) d -> p c d", c=CHUNKS)[:, chunks, :], in_=rows[:])

        noise_t = keep.tile([P, ROWS], F32)
        y_t = keep.tile([P, ROWS], F32)
        z_t = keep.tile([P, ROWS], F32)
        zx_t = keep.tile([P, ROWS], F32)
        bank_cols = [slice(b * BANK, (b + 1) * BANK) for b in range(BANKS)]

        lv_mean_var, lv_shifted, lv_half_inv = mean_and_inverse_std(LOGVAR, stats[:, LOGVAR], BN_EPS, 4.0)
        lv_minus_mean = keep.tile([P, 1], F32)
        nc.vector.tensor_scalar_mul(out=lv_minus_mean[:], in0=lv_mean_var[:, 0:1], scalar1=-1.0)
        exp_bias = keep.tile([P, 1], F32)
        nc.scalar.activation(out=exp_bias[:], in_=lv_minus_mean[:], func=ACT.Copy, scale=lv_half_inv[:])
        for b in range(BANKS):
            nc.scalar.activation(
                out=noise_t[:, bank_cols[b]],
                in_=head_out[(LOGVAR, b)][:],
                func=ACT.Exp,
                bias=exp_bias[:],
                scale=lv_half_inv[:],
            )

        for b in range(BANKS):
            nc.vector.bn_stats(out=stats[:, MEAN, b, :], in_=head_out[(MEAN, b)][:])
        m_mean_var, m_shifted, m_inv = mean_and_inverse_std(MEAN, stats[:, MEAN], BN_EPS, 1.0)
        for b in range(BANKS):
            chunks = slice(b * CHUNKS_PER_BANK, (b + 1) * CHUNKS_PER_BANK)
            nc.vector.tensor_tensor(
                out=noise_t[:, bank_cols[b]],
                in0=noise_t[:, bank_cols[b]],
                in1=eps_flipped[:, chunks, :].rearrange("d c n -> d (c n)"),
                op=ALU.mult,
            )
        m_sd = keep.tile([P, 1], F32)
        nc.vector.tensor_tensor(out=m_sd[:], in0=m_shifted[:], in1=m_inv[:], op=ALU.mult)
        y_epsilon = keep.tile([P, 1], F32)
        nc.vector.tensor_scalar_mul(out=y_epsilon[:], in0=m_shifted[:], scalar1=BN_EPS)
        z_bias = keep.tile([P, 1], F32)
        nc.vector.scalar_tensor_tensor(
            out=z_bias[:], in0=m_mean_var[:, 0:1], scalar=-1.0, in1=m_inv[:], op0=ALU.mult, op1=ALU.mult
        )
        for b in range(BANKS):
            nc.vector.scalar_tensor_tensor(
                out=y_t[:, bank_cols[b]],
                in0=noise_t[:, bank_cols[b]],
                scalar=m_sd[:],
                in1=head_out[(MEAN, b)][:],
                op0=ALU.mult,
                op1=ALU.add,
            )
            nc.vector.bn_stats(out=stats[:, SAMPLE, b, :], in_=y_t[:, bank_cols[b]])
            nc.scalar.activation(
                out=z_t[:, bank_cols[b]], in_=y_t[:, bank_cols[b]], func=ACT.Identity, bias=z_bias[:], scale=m_inv[:]
            )
            store_rows(z_t, b, nc.scalar.copy, out_0)

        y_mean_var, y_shifted, y_inv = mean_and_inverse_std(SAMPLE, stats[:, SAMPLE], y_epsilon[:], 1.0)
        for b in range(BANKS):
            nc.vector.tensor_scalar(
                out=zx_t[:, bank_cols[b]],
                in0=y_t[:, bank_cols[b]],
                scalar1=y_mean_var[:, 0:1],
                scalar2=y_inv[:],
                op0=ALU.subtract,
                op1=ALU.mult,
            )
        store_rows(zx_t, 0, nc.scalar.copy, out_1)
        store_rows(zx_t, 1, nc.vector.tensor_copy, out_1)
